import numpy as np
import ml_dtypes


def mxq(x, axis, fmt="e4m3"):
    dtype, down = {"e4m3": (ml_dtypes.float8_e4m3fn, 7), "e5m2": (ml_dtypes.float8_e5m2, 14)}[fmt]
    v = np.moveaxis(np.asarray(x, np.float32).astype(ml_dtypes.bfloat16).astype(np.float64), axis, -1)
    blocks = v.reshape(v.shape[:-1] + (-1, 32))
    amax = np.abs(blocks).max(-1, keepdims=True)
    byte = np.maximum(np.where(amax > 0, np.frexp(amax)[1] - 1 + 127, 0) - down, 1)
    scale = np.exp2(byte - 127.0)
    codes = (blocks / scale).astype(np.float32).astype(dtype).astype(np.float64)
    return np.moveaxis((codes * scale).reshape(v.shape), -1, axis)


WIDE = False


def mx_kscale(k):
    if not WIDE:
        return np.ones(k)
    levels = np.array([10, -10, 5, -5, 0])
    if k % 512:
        return np.exp2(np.random.permutation(np.resize(levels, k // 32))).repeat(32)
    a = np.empty((k // 512, 16))
    for p in range(k // 512):
        a[p, :8] = np.random.permutation(np.resize(levels, 8))
        for g in range(8):
            far = levels[np.abs(levels - a[p, g]) >= 10]
            a[p, g + 8] = far[np.random.randint(len(far))]
    return np.exp2(a.ravel()).repeat(32)


BF16 = ml_dtypes.bfloat16


def bf(x):
    return np.asarray(x, np.float32).astype(BF16)


def f64(x):
    return np.asarray(x).astype(np.float64)


B, N, D, NFF = 128, 1024, 8, 1024
KI = D * N
ALPHA = 0.95
RHO = 0.9
BETA = 1.8
TH = 1.0
P = 0.1
GAP = 0.0625


def spikes(shape):
    return (np.random.random_sample(shape) < P) * (1.0 + 0.25 * np.random.standard_normal(shape))


def setup_inputs():
    s = mx_kscale(KI).reshape(D, N)
    u = mx_kscale(NFF)
    a = bf(np.random.random_sample((B, N)))
    theta = TH + BETA * f64(a)
    d = 1.0 + 1.5 * np.random.standard_normal((B, N)) - theta
    V = bf(theta + d + GAP * np.sign(d))
    return {"FF": bf(spikes((B, NFF)) * u),
            "V": V,
            "a": a,
            "Xd": bf(spikes((D, B, N)) * s[:, None, :]),
            "W_int": bf(np.random.standard_normal((D, N, N)) * 0.8 / np.sqrt(P * KI) / s[:, :, None]),
            "W_ff": bf(np.random.standard_normal((NFF, N)) * 0.8 / np.sqrt(P * NFF) / u[:, None])}


def core(FF, V, a, Xd, W_int, W_ff):
    FF, V, a, Xd, W_int, W_ff = f64(FF), f64(V), f64(a), f64(Xd), f64(W_int), f64(W_ff)
    theta = TH + BETA * a
    X = (V - theta > 0).astype(np.float64)
    xq = mxq(Xd.transpose(1, 0, 2).reshape(B, KI), 1, "e4m3")
    wq = mxq(W_int.reshape(KI, N), 0, "e4m3")
    I_int = xq @ wq
    I_ff = mxq(FF, 1, "e4m3") @ mxq(W_ff, 0, "e4m3")
    current = I_int + I_ff
    V_new = ALPHA * V * (1.0 - X) + current
    a_new = RHO * a + X
    return np.stack([X, V_new, a_new])


def e4m3fn_bytes(y):
    return np.clip(np.asarray(y, np.float64), -448.0, 448.0).astype(np.float32).astype(ml_dtypes.float8_e4m3fn).view(np.uint8)


Y_SCALE = 190.0


def reference(FF, V, a, Xd, W_int, W_ff):
    out = core(FF, V, a, Xd, W_int, W_ff)
    return out, e4m3fn_bytes(out * Y_SCALE)

@@ -1,0 +1,261 @@
+from contextlib import ExitStack
+
+import concourse.masks as masks
+import concourse.mybir as mybir
+
+FLOPS = 2 * 128 * 9216 * 1024
+
+F32 = mybir.dt.float32
+BF16 = mybir.dt.bfloat16
+U32 = mybir.dt.uint32
+U8 = mybir.dt.uint8
+FP8X4 = mybir.dt.float8_e4m3fn_x4
+FP8 = mybir.dt.float8_e4m3fn
+ALU = mybir.AluOpType
+COPY = mybir.ActivationFunctionType.Copy
+
+P = 128
+PACK = 4
+K_PASS = P * PACK
+N_OUT = 1024
+N_GRP = 256
+PASSES = 18
+PAIRS = PASSES // 2
+EDGE = 256
+FORM_B = True
+V_FULL = 520
+V_EDGE = 120
+RAW_BUFS = 10
+
+
+def make_units():
+    units = []
+    for g in range(PASSES):
+        if g == 0 or g == PASSES - 1:
+            for m0 in range(0, N_OUT, EDGE):
+                units.append((g, m0, EDGE, V_EDGE))
+        else:
+            units.append((g, 0, N_OUT, V_FULL))
+    return units
+
+
+def tile_snn_kernel(tc, FF, V, a, Xd, W_int, W_ff, out_0, out_1):
+    nc = tc.nc
+    units = make_units()
+    n_units = len(units)
+    first_unit = {}
+    for i, u in enumerate(units):
+        first_unit.setdefault(u[0], i)
+
+    with ExitStack() as ctx:
+        const = ctx.enter_context(tc.tile_pool(name="const", bufs=1))
+        raw_full = ctx.enter_context(tc.tile_pool(name="raw_full", bufs=RAW_BUFS))
+        raw_edge = ctx.enter_context(tc.tile_pool(name="raw_edge", bufs=4))
+        grp_pool = ctx.enter_context(tc.tile_pool(name="grp", bufs=3))
+        wq_pool = ctx.enter_context(tc.tile_pool(name="wq", bufs=3))
+        xr_pool = ctx.enter_context(tc.tile_pool(name="xr", bufs=4))
+        xg_pool = ctx.enter_context(tc.tile_pool(name="xg", bufs=2))
+        xq_pool = ctx.enter_context(tc.tile_pool(name="xq", bufs=3))
+        acc_pool = ctx.enter_context(tc.psum_pool(name="acc", bufs=1))
+        xt_pool = ctx.enter_context(tc.psum_pool(name="xt", bufs=2))
+        ctx.enter_context(tc.manual_schedule())
+
+        raw = {}
+        grouped = {}
+        w_codes = {}
+        w_scales = {}
+        x_raw = {}
+        x_t = {}
+        x_grp = {}
+        x_codes = {}
+        x_scales = {}
+
+        def w_rows(g):
+            if g < 16:
+                return W_int[g // 2, K_PASS * (g % 2) : K_PASS * (g % 2 + 1), :]
+            return W_ff[K_PASS * (g - 16) : K_PASS * (g - 15), :]
+
+        def load_w(i):
+            g, m0, width, v_cols = units[i]
+            pool = raw_full if width == N_OUT else raw_edge
+            t = pool.tile([P, PACK, width], BF16, name="raw")
+            nc.sync.dma_start(
+                out=t[:],
+                in_=w_rows(g).rearrange("(p j) m -> p j m", j=PACK)[:, :, m0 : m0 + width],
+            )
+            raw[i] = t
+
+        def load_x(d):
+            t = xr_pool.tile([P, N_OUT], BF16, name="xr")
+            nc.sync.dma_start(out=t[:], in_=(Xd[d] if d < 8 else FF))
+            x_raw[d] = t
+
+        def interleave(copy, dst, src, lo, hi):
+            if hi <= lo:
+                return
+            if FORM_B:
+                copy(
+                    out=dst[:, lo:hi, :].rearrange("p (c i) t -> p c t i", i=4),
+                    in_=src[:, :, lo:hi].rearrange("p t (c i) -> p c t i", i=4),
+                )
+            else:
+                copy(out=dst[:, lo:hi, :], in_=src[:, :, lo:hi].rearrange("p t m -> p m t"))
+
+        def copy_w(i):
+            g, m0, width, v_cols = units[i]
+            t = grp_pool.tile([P, width, PACK], BF16, name="grp", align_bytes=64)
+            interleave(nc.vector.tensor_copy, t, raw[i], 0, v_cols)
+            interleave(nc.scalar.copy, t, raw[i], v_cols, width)
+            grouped[i] = t
+
+        def quant_w(i):
+            g, m0, width, v_cols = units[i]
+            c = wq_pool.tile([P, width], U32, name="wc", align_bytes=64)
+            s = wq_pool.tile([P, width], U8, name="ws", align_bytes=64)
+            nc.vector.quantize_mx(
+                out=c[:].bitcast(FP8X4),
+                scales=s[:],
+                in_=grouped[i][:].rearrange("p m j -> p (m j)"),
+            )
+            w_codes[i] = c
+            w_scales[i] = s
+
+        def mm(i):
+            g, m0, width, v_cols = units[i]
+            d, h = g // 2, g % 2
+            b_cols = slice(P * h, P * (h + 1))
+            for n0 in range(0, width, N_GRP):
+                n_cols = slice(n0, n0 + N_GRP)
+                nc.tensor.matmul_mx(
+                    out=acc[(m0 + n0) // N_GRP][:],
+                    lhsT=x_codes[d][:, b_cols].bitcast(FP8X4),
+                    lhsT_scale=x_scales[d][:, b_cols],
+                    rhs=w_codes[i][:, n_cols].bitcast(FP8X4),
+                    rhs_scale=w_scales[i][:, n_cols],
+                    start=(g == 0),
+                    stop=(g == PASSES - 1),
+                )
+
+        def xpose(d):
+            t = xt_pool.tile([P, 2, 2, P], F32, name="xt")
+            words = x_raw[d][:].bitcast(F32)
+            for h in range(2):
+                for u in range(2):
+                    nc.tensor.transpose(
+                        t[:, h, u, :], words[:, 256 * h + u : 256 * (h + 1) : 2], ident[:]
+                    )
+            x_t[d] = t
+
+        def xevac(d):
+            t = xg_pool.tile([P, 2, P, PACK], BF16, name="xg", align_bytes=64)
+            nc.scalar.copy(out=t[:].bitcast(F32), in_=x_t[d][:].rearrange("p h u b -> p h b u"))
+            x_grp[d] = t
+
+        def xquant(d):
+            c = xq_pool.tile([P, 2 * P], U32, name="xc", align_bytes=64)
+            s = xq_pool.tile([P, 2 * P], U8, name="xs", align_bytes=64)
+            nc.vector.quantize_mx(
+                out=c[:].bitcast(FP8X4),
+                scales=s[:],
+                in_=x_grp[d][:].rearrange("p h b t -> p (h b t)"),
+            )
+            x_codes[d] = c
+            x_scales[d] = s
+
+        warm = const.tile([P, 1], F32, name="warm")
+        nc.gpsimd.memset(warm[:], 0.0)
+        warm2 = const.tile([P, 1], F32, name="warm2")
+        nc.scalar.activation(out=warm2[:], in_=warm[:], func=COPY, scale=1.0)
+        ident = const.tile([P, P], F32, name="ident")
+        masks.make_identity(nc, ident[:])
+
+        acc = []
+        for q in range(N_OUT // N_GRP):
+            acc_q = acc_pool.tile([P, N_GRP], F32, name="acc%d" % q)
+            acc.append(acc_q)
+
+        a_sb = const.tile([P, N_OUT], BF16, name="a_sb")
+        v_sb = const.tile([P, N_OUT], BF16, name="v_sb")
+        dist = const.tile([P, N_OUT], F32, name="dist")
+        spike = const.tile([P, N_OUT], F32, name="spike")
+        v_keep = const.tile([P, N_OUT], F32, name="v_keep")
+        a_new = const.tile([P, N_OUT], F32, name="a_new")
+        v_new = const.tile([P, N_OUT], F32, name="v_new")
+        spike8 = const.tile([P, N_OUT], FP8, name="spike8")
+        a_new8 = const.tile([P, N_OUT], FP8, name="a_new8")
+        v_new8 = const.tile([P, N_OUT], FP8, name="v_new8")
+
+        load_w(0)
+        nc.sync.dma_start(out=a_sb[:], in_=a)
+        nc.sync.dma_start(out=v_sb[:], in_=V)
+        load_w(1)
+        load_x(0)
+        for i in range(2, n_units):
+            if i % 2 == 0 and i // 2 < PAIRS:
+                load_x(i // 2)
+            load_w(i)
+
+        def pre(k):
+            if k == 0:
+                nc.vector.scalar_tensor_tensor(
+                    out=dist[:], in0=a_sb[:], scalar=-1.8, in1=v_sb[:], op0=ALU.mult, op1=ALU.add
+                )
+            elif k == 1:
+                nc.vector.tensor_scalar(
+                    out=spike[:], in0=dist[:], scalar1=1.0, scalar2=None, op0=ALU.is_gt
+                )
+            elif k == 2:
+                nc.vector.scalar_tensor_tensor(
+                    out=v_keep[:], in0=dist[:], scalar=1.0, in1=v_sb[:], op0=ALU.is_le, op1=ALU.mult
+                )
+            elif k == 3:
+                nc.vector.scalar_tensor_tensor(
+                    out=a_new[:], in0=a_sb[:], scalar=0.9, in1=spike[:], op0=ALU.mult, op1=ALU.add
+                )
+
+        def cast_store(plane, val, val8, cols):
+            nc.scalar.activation(
+                out=val8[:, cols], in_=val[:, cols], func=COPY, scale=190.0, saturate=False
+            )
+            nc.sync.dma_start(out=out_0[plane][:, cols], in_=val[:, cols])
+            nc.sync.dma_start(out=out_1[plane][:, cols], in_=val8[:, cols].bitcast(U8))
+
+        def finish(i):
+            g, m0, width, v_cols = units[i]
+            cols = slice(m0, m0 + width)
+            nc.vector.scalar_tensor_tensor(
+                out=v_new[:, cols],
+                in0=v_keep[:, cols],
+                scalar=0.95,
+                in1=acc[m0 // N_GRP][:],
+                op0=ALU.mult,
+                op1=ALU.add,
+            )
+            cast_store(1, v_new, v_new8, cols)
+
+        whole = slice(0, N_OUT)
+        for step in range(n_units + 2):
+            if step < n_units:
+                copy_w(step)
+            if step == 1:
+                xpose(0)
+                xevac(0)
+                xquant(0)
+            for d in range(1, PAIRS):
+                if step == first_unit[2 * d] - 2:
+                    xpose(d)
+                if step == first_unit[2 * d] - 1:
+                    xevac(d)
+                if step == first_unit[2 * d]:
+                    xquant(d)
+            if 2 <= step < 6:
+                pre(step - 2)
+            if step == 7:
+                cast_store(0, spike, spike8, whole)
+            if step == 8:
+                cast_store(2, a_new, a_new8, whole)
+            if 1 <= step <= n_units:
+                quant_w(step - 1)
+                mm(step - 1)
+            if step >= 2 and units[step - 2][0] == PASSES - 1:
+                finish(step - 2)

@@ -21,21 +21,17 @@ N_OUT = 1024
 N_GRP = 256
 PASSES = 18
 PAIRS = PASSES // 2
-EDGE = 256
-FORM_B = True
-V_FULL = 520
-V_EDGE = 120
 RAW_BUFS = 10
+FIN_LAG = 3
+CAST_SPIKE_STEP = 18
+CAST_A_STEP = 1
 
 
 def make_units():
-    units = []
-    for g in range(PASSES):
-        if g == 0 or g == PASSES - 1:
-            for m0 in range(0, N_OUT, EDGE):
-                units.append((g, m0, EDGE, V_EDGE))
-        else:
-            units.append((g, 0, N_OUT, V_FULL))
+    units = [(0, 0, 1024, 512)]
+    for g in range(1, PASSES - 1):
+        units.append((g, 0, N_OUT, 504))
+    units.extend([(17, 0, 512, 136), (17, 512, 512, 248)])
     return units
 
 
@@ -49,10 +45,9 @@ def tile_snn_kernel(tc, FF, V, a, Xd, W_int, W_ff, out_0, out_1):
 
     with ExitStack() as ctx:
         const = ctx.enter_context(tc.tile_pool(name="const", bufs=1))
-        raw_full = ctx.enter_context(tc.tile_pool(name="raw_full", bufs=RAW_BUFS))
-        raw_edge = ctx.enter_context(tc.tile_pool(name="raw_edge", bufs=4))
+        raw_pool = ctx.enter_context(tc.tile_pool(name="raw", bufs=RAW_BUFS))
         grp_pool = ctx.enter_context(tc.tile_pool(name="grp", bufs=3))
-        wq_pool = ctx.enter_context(tc.tile_pool(name="wq", bufs=3))
+        wq_pool = ctx.enter_context(tc.tile_pool(name="wq", bufs=4))
         xr_pool = ctx.enter_context(tc.tile_pool(name="xr", bufs=4))
         xg_pool = ctx.enter_context(tc.tile_pool(name="xg", bufs=2))
         xq_pool = ctx.enter_context(tc.tile_pool(name="xq", bufs=3))
@@ -70,46 +65,36 @@ def tile_snn_kernel(tc, FF, V, a, Xd, W_int, W_ff, out_0, out_1):
         x_codes = {}
         x_scales = {}
 
-        def w_rows(g):
+        def load_w(g):
             if g < 16:
-                return W_int[g // 2, K_PASS * (g % 2) : K_PASS * (g % 2 + 1), :]
-            return W_ff[K_PASS * (g - 16) : K_PASS * (g - 15), :]
-
-        def load_w(i):
-            g, m0, width, v_cols = units[i]
-            pool = raw_full if width == N_OUT else raw_edge
-            t = pool.tile([P, PACK, width], BF16, name="raw")
-            nc.sync.dma_start(
-                out=t[:],
-                in_=w_rows(g).rearrange("(p j) m -> p j m", j=PACK)[:, :, m0 : m0 + width],
-            )
-            raw[i] = t
+                rows = W_int[g // 2, K_PASS * (g % 2) : K_PASS * (g % 2 + 1), :]
+            else:
+                rows = W_ff[K_PASS * (g - 16) : K_PASS * (g - 15), :]
+            t = raw_pool.tile([P, PACK, N_OUT], BF16, name="raw")
+            nc.sync.dma_start(out=t[:], in_=rows.rearrange("(p j) m -> p j m", j=PACK))
+            raw[g] = t
 
         def load_x(d):
             t = xr_pool.tile([P, N_OUT], BF16, name="xr")
             nc.sync.dma_start(out=t[:], in_=(Xd[d] if d < 8 else FF))
             x_raw[d] = t
 
-        def interleave(copy, dst, src, lo, hi):
-            if hi <= lo:
-                return
-            if FORM_B:
+        def interleave(copy, dst, src, m0, lo, hi):
+            if hi > lo:
                 copy(
                     out=dst[:, lo:hi, :].rearrange("p (c i) t -> p c t i", i=4),
-                    in_=src[:, :, lo:hi].rearrange("p t (c i) -> p c t i", i=4),
+                    in_=src[:, :, m0 + lo : m0 + hi].rearrange("p t (c i) -> p c t i", i=4),
                 )
-            else:
-                copy(out=dst[:, lo:hi, :], in_=src[:, :, lo:hi].rearrange("p t m -> p m t"))
 
         def copy_w(i):
             g, m0, width, v_cols = units[i]
             t = grp_pool.tile([P, width, PACK], BF16, name="grp", align_bytes=64)
-            interleave(nc.vector.tensor_copy, t, raw[i], 0, v_cols)
-            interleave(nc.scalar.copy, t, raw[i], v_cols, width)
+            interleave(nc.vector.tensor_copy, t, raw[g], m0, 0, v_cols)
+            interleave(nc.scalar.copy, t, raw[g], m0, v_cols, width)
             grouped[i] = t
 
         def quant_w(i):
-            g, m0, width, v_cols = units[i]
+            width = units[i][2]
             c = wq_pool.tile([P, width], U32, name="wc", align_bytes=64)
             s = wq_pool.tile([P, width], U8, name="ws", align_bytes=64)
             nc.vector.quantize_mx(
@@ -185,33 +170,25 @@ def tile_snn_kernel(tc, FF, V, a, Xd, W_int, W_ff, out_0, out_1):
         a_new8 = const.tile([P, N_OUT], FP8, name="a_new8")
         v_new8 = const.tile([P, N_OUT], FP8, name="v_new8")
 
-        load_w(0)
         nc.sync.dma_start(out=a_sb[:], in_=a)
         nc.sync.dma_start(out=v_sb[:], in_=V)
-        load_w(1)
+        load_w(0)
         load_x(0)
-        for i in range(2, n_units):
-            if i % 2 == 0 and i // 2 < PAIRS:
-                load_x(i // 2)
-            load_w(i)
+        for g in range(1, PASSES):
+            if g % 2 == 0:
+                load_x(g // 2)
+            load_w(g)
 
-        def pre(k):
-            if k == 0:
-                nc.vector.scalar_tensor_tensor(
-                    out=dist[:], in0=a_sb[:], scalar=-1.8, in1=v_sb[:], op0=ALU.mult, op1=ALU.add
-                )
-            elif k == 1:
-                nc.vector.tensor_scalar(
-                    out=spike[:], in0=dist[:], scalar1=1.0, scalar2=None, op0=ALU.is_gt
-                )
-            elif k == 2:
-                nc.vector.scalar_tensor_tensor(
-                    out=v_keep[:], in0=dist[:], scalar=1.0, in1=v_sb[:], op0=ALU.is_le, op1=ALU.mult
-                )
-            elif k == 3:
-                nc.vector.scalar_tensor_tensor(
-                    out=a_new[:], in0=a_sb[:], scalar=0.9, in1=spike[:], op0=ALU.mult, op1=ALU.add
-                )
+        nc.vector.scalar_tensor_tensor(
+            out=dist[:], in0=a_sb[:], scalar=-1.8, in1=v_sb[:], op0=ALU.mult, op1=ALU.add
+        )
+        nc.vector.tensor_scalar(out=spike[:], in0=dist[:], scalar1=1.0, scalar2=None, op0=ALU.is_gt)
+        nc.vector.scalar_tensor_tensor(
+            out=v_keep[:], in0=dist[:], scalar=1.0, in1=v_sb[:], op0=ALU.is_le, op1=ALU.mult
+        )
+        nc.vector.scalar_tensor_tensor(
+            out=a_new[:], in0=a_sb[:], scalar=0.9, in1=spike[:], op0=ALU.mult, op1=ALU.add
+        )
 
         def cast_store(plane, val, val8, cols):
             nc.scalar.activation(
@@ -222,40 +199,33 @@ def tile_snn_kernel(tc, FF, V, a, Xd, W_int, W_ff, out_0, out_1):
 
         def finish(i):
             g, m0, width, v_cols = units[i]
-            cols = slice(m0, m0 + width)
-            nc.vector.scalar_tensor_tensor(
-                out=v_new[:, cols],
-                in0=v_keep[:, cols],
-                scalar=0.95,
-                in1=acc[m0 // N_GRP][:],
-                op0=ALU.mult,
-                op1=ALU.add,
-            )
-            cast_store(1, v_new, v_new8, cols)
+            for n0 in range(m0, m0 + width, N_GRP):
+                nc.vector.scalar_tensor_tensor(
+                    out=v_new[:, n0 : n0 + N_GRP],
+                    in0=v_keep[:, n0 : n0 + N_GRP],
+                    scalar=0.95,
+                    in1=acc[n0 // N_GRP][:],
+                    op0=ALU.mult,
+                    op1=ALU.add,
+                )
+            cast_store(1, v_new, v_new8, slice(m0, m0 + width))
 
         whole = slice(0, N_OUT)
-        for step in range(n_units + 2):
+        for step in range(n_units + FIN_LAG + 1):
             if step < n_units:
                 copy_w(step)
-            if step == 1:
-                xpose(0)
-                xevac(0)
-                xquant(0)
-            for d in range(1, PAIRS):
-                if step == first_unit[2 * d] - 2:
-                    xpose(d)
-                if step == first_unit[2 * d] - 1:
-                    xevac(d)
+            for d in range(PAIRS):
                 if step == first_unit[2 * d]:
+                    xpose(d)
+                    xevac(d)
+                if step == first_unit[2 * d] + 1:
                     xquant(d)
-            if 2 <= step < 6:
-                pre(step - 2)
-            if step == 7:
+            if step == CAST_SPIKE_STEP:
                 cast_store(0, spike, spike8, whole)
-            if step == 8:
+            if step == CAST_A_STEP:
                 cast_store(2, a_new, a_new8, whole)
             if 1 <= step <= n_units:
                 quant_w(step - 1)
                 mm(step - 1)
-            if step >= 2 and units[step - 2][0] == PASSES - 1:
-                finish(step - 2)
+            if FIN_LAG <= step < n_units + FIN_LAG and units[step - FIN_LAG][0] == PASSES - 1:
+                finish(step - FIN_LAG)

@@ -23,6 +23,8 @@ PASSES = 18
 PAIRS = PASSES // 2
 RAW_BUFS = 10
 FIN_LAG = 3
+PE_PASSES = (2, 4, 6, 8, 10, 12, 14)
+PE_COLS = 256
 CAST_SPIKE_STEP = 18
 CAST_A_STEP = 1
 
@@ -53,9 +55,11 @@ def tile_snn_kernel(tc, FF, V, a, Xd, W_int, W_ff, out_0, out_1):
         xq_pool = ctx.enter_context(tc.tile_pool(name="xq", bufs=3))
         acc_pool = ctx.enter_context(tc.psum_pool(name="acc", bufs=1))
         xt_pool = ctx.enter_context(tc.psum_pool(name="xt", bufs=2))
+        pw_pool = ctx.enter_context(tc.psum_pool(name="pw", bufs=2))
         ctx.enter_context(tc.manual_schedule())
 
         raw = {}
+        laid = {}
         grouped = {}
         w_codes = {}
         w_scales = {}
@@ -86,11 +90,29 @@ def tile_snn_kernel(tc, FF, V, a, Xd, W_int, W_ff, out_0, out_1):
                     in_=src[:, :, m0 + lo : m0 + hi].rearrange("p t (c i) -> p c t i", i=4),
                 )
 
+        def lay_w(i):
+            g, m0, width, v_cols = units[i]
+            if g in PE_PASSES:
+                t = pw_pool.tile([P, PE_COLS, PACK], BF16, name="pw")
+                for c0 in range(0, PE_COLS, P):
+                    m1 = m0 + width - PE_COLS + c0
+                    nc.tensor.matmul(
+                        out=t[:, c0 : c0 + P, :],
+                        lhsT=ident_bf[:],
+                        rhs=raw[g][:, :, m1 : m1 + P].rearrange("p t m -> p m t"),
+                        start=True,
+                        stop=True,
+                    )
+                laid[i] = t
+
         def copy_w(i):
             g, m0, width, v_cols = units[i]
             t = grp_pool.tile([P, width, PACK], BF16, name="grp", align_bytes=64)
+            s_end = width - PE_COLS if g in PE_PASSES else width
             interleave(nc.vector.tensor_copy, t, raw[g], m0, 0, v_cols)
-            interleave(nc.scalar.copy, t, raw[g], m0, v_cols, width)
+            interleave(nc.scalar.copy, t, raw[g], m0, v_cols, s_end)
+            if s_end < width:
+                nc.scalar.copy(out=t[:, s_end:width, :], in_=laid[i][:])
             grouped[i] = t
 
         def quant_w(i):
@@ -153,6 +175,8 @@ def tile_snn_kernel(tc, FF, V, a, Xd, W_int, W_ff, out_0, out_1):
         nc.scalar.activation(out=warm2[:], in_=warm[:], func=COPY, scale=1.0)
         ident = const.tile([P, P], F32, name="ident")
         masks.make_identity(nc, ident[:])
+        ident_bf = const.tile([P, P], BF16, name="ident_bf")
+        masks.make_identity(nc, ident_bf[:])
 
         acc = []
         for q in range(N_OUT // N_GRP):
@@ -212,6 +236,8 @@ def tile_snn_kernel(tc, FF, V, a, Xd, W_int, W_ff, out_0, out_1):
 
         whole = slice(0, N_OUT)
         for step in range(n_units + FIN_LAG + 1):
+            if step + 1 < n_units:
+                lay_w(step + 1)
             if step < n_units:
                 copy_w(step)
             for d in range(PAIRS):

@@ -23,8 +23,6 @@ PASSES = 18
 PAIRS = PASSES // 2
 RAW_BUFS = 10
 FIN_LAG = 3
-PE_PASSES = (2, 4, 6, 8, 10, 12, 14)
-PE_COLS = 256
 CAST_SPIKE_STEP = 18
 CAST_A_STEP = 1
 
@@ -32,7 +30,7 @@ CAST_A_STEP = 1
 def make_units():
     units = [(0, 0, 1024, 512)]
     for g in range(1, PASSES - 1):
-        units.append((g, 0, N_OUT, 504))
+        units.append((g, 0, N_OUT, 544))
     units.extend([(17, 0, 512, 136), (17, 512, 512, 248)])
     return units
 
@@ -55,11 +53,9 @@ def tile_snn_kernel(tc, FF, V, a, Xd, W_int, W_ff, out_0, out_1):
         xq_pool = ctx.enter_context(tc.tile_pool(name="xq", bufs=3))
         acc_pool = ctx.enter_context(tc.psum_pool(name="acc", bufs=1))
         xt_pool = ctx.enter_context(tc.psum_pool(name="xt", bufs=2))
-        pw_pool = ctx.enter_context(tc.psum_pool(name="pw", bufs=2))
         ctx.enter_context(tc.manual_schedule())
 
         raw = {}
-        laid = {}
         grouped = {}
         w_codes = {}
         w_scales = {}
@@ -90,29 +86,11 @@ def tile_snn_kernel(tc, FF, V, a, Xd, W_int, W_ff, out_0, out_1):
                     in_=src[:, :, m0 + lo : m0 + hi].rearrange("p t (c i) -> p c t i", i=4),
                 )
 
-        def lay_w(i):
-            g, m0, width, v_cols = units[i]
-            if g in PE_PASSES:
-                t = pw_pool.tile([P, PE_COLS, PACK], BF16, name="pw")
-                for c0 in range(0, PE_COLS, P):
-                    m1 = m0 + width - PE_COLS + c0
-                    nc.tensor.matmul(
-                        out=t[:, c0 : c0 + P, :],
-                        lhsT=ident_bf[:],
-                        rhs=raw[g][:, :, m1 : m1 + P].rearrange("p t m -> p m t"),
-                        start=True,
-                        stop=True,
-                    )
-                laid[i] = t
-
         def copy_w(i):
             g, m0, width, v_cols = units[i]
             t = grp_pool.tile([P, width, PACK], BF16, name="grp", align_bytes=64)
-            s_end = width - PE_COLS if g in PE_PASSES else width
             interleave(nc.vector.tensor_copy, t, raw[g], m0, 0, v_cols)
-            interleave(nc.scalar.copy, t, raw[g], m0, v_cols, s_end)
-            if s_end < width:
-                nc.scalar.copy(out=t[:, s_end:width, :], in_=laid[i][:])
+            interleave(nc.scalar.copy, t, raw[g], m0, v_cols, width)
             grouped[i] = t
 
         def quant_w(i):
@@ -175,8 +153,6 @@ def tile_snn_kernel(tc, FF, V, a, Xd, W_int, W_ff, out_0, out_1):
         nc.scalar.activation(out=warm2[:], in_=warm[:], func=COPY, scale=1.0)
         ident = const.tile([P, P], F32, name="ident")
         masks.make_identity(nc, ident[:])
-        ident_bf = const.tile([P, P], BF16, name="ident_bf")
-        masks.make_identity(nc, ident_bf[:])
 
         acc = []
         for q in range(N_OUT // N_GRP):
@@ -236,8 +212,6 @@ def tile_snn_kernel(tc, FF, V, a, Xd, W_int, W_ff, out_0, out_1):
 
         whole = slice(0, N_OUT)
         for step in range(n_units + FIN_LAG + 1):
-            if step + 1 < n_units:
-                lay_w(step + 1)
             if step < n_units:
                 copy_w(step)
             for d in range(PAIRS):

@@ -23,15 +23,15 @@ PASSES = 18
 PAIRS = PASSES // 2
 RAW_BUFS = 10
 FIN_LAG = 3
-CAST_SPIKE_STEP = 18
+CAST_SPIKE_STEP = 2
 CAST_A_STEP = 1
 
 
 def make_units():
     units = [(0, 0, 1024, 512)]
     for g in range(1, PASSES - 1):
-        units.append((g, 0, N_OUT, 544))
-    units.extend([(17, 0, 512, 136), (17, 512, 512, 248)])
+        units.append((g, 0, N_OUT, 536))
+    units.extend([(17, 0, 256, 64), (17, 256, 256, 64), (17, 512, 256, 64), (17, 768, 256, 104)])
     return units
 
 

from contextlib import ExitStack

import concourse.masks as masks
import concourse.mybir as mybir

FLOPS = 2 * 128 * 9216 * 1024

F32 = mybir.dt.float32
BF16 = mybir.dt.bfloat16
U32 = mybir.dt.uint32
U8 = mybir.dt.uint8
FP8X4 = mybir.dt.float8_e4m3fn_x4
FP8 = mybir.dt.float8_e4m3fn
ALU = mybir.AluOpType
COPY = mybir.ActivationFunctionType.Copy

P = 128
PACK = 4
K_PASS = P * PACK
N_OUT = 1024
N_GRP = 256
PASSES = 18
PAIRS = PASSES // 2
RAW_BUFS = 10
FIN_LAG = 3
CAST_SPIKE_STEP = 2
CAST_A_STEP = 1


def make_units():
    units = [(0, 0, 1024, 512)]
    for g in range(1, PASSES - 1):
        units.append((g, 0, N_OUT, 536))
    units.extend([(17, 0, 256, 64), (17, 256, 256, 64), (17, 512, 256, 64), (17, 768, 256, 104)])
    return units


def tile_snn_kernel(tc, FF, V, a, Xd, W_int, W_ff, out_0, out_1):
    nc = tc.nc
    units = make_units()
    n_units = len(units)
    first_unit = {}
    for i, u in enumerate(units):
        first_unit.setdefault(u[0], i)

    with ExitStack() as ctx:
        const = ctx.enter_context(tc.tile_pool(name="const", bufs=1))
        raw_pool = ctx.enter_context(tc.tile_pool(name="raw", bufs=RAW_BUFS))
        grp_pool = ctx.enter_context(tc.tile_pool(name="grp", bufs=3))
        wq_pool = ctx.enter_context(tc.tile_pool(name="wq", bufs=4))
        xr_pool = ctx.enter_context(tc.tile_pool(name="xr", bufs=4))
        xg_pool = ctx.enter_context(tc.tile_pool(name="xg", bufs=2))
        xq_pool = ctx.enter_context(tc.tile_pool(name="xq", bufs=3))
        acc_pool = ctx.enter_context(tc.psum_pool(name="acc", bufs=1))
        xt_pool = ctx.enter_context(tc.psum_pool(name="xt", bufs=2))
        ctx.enter_context(tc.manual_schedule())

        raw = {}
        grouped = {}
        w_codes = {}
        w_scales = {}
        x_raw = {}
        x_t = {}
        x_grp = {}
        x_codes = {}
        x_scales = {}

        def load_w(g):
            if g < 16:
                rows = W_int[g // 2, K_PASS * (g % 2) : K_PASS * (g % 2 + 1), :]
            else:
                rows = W_ff[K_PASS * (g - 16) : K_PASS * (g - 15), :]
            t = raw_pool.tile([P, PACK, N_OUT], BF16, name="raw")
            nc.sync.dma_start(out=t[:], in_=rows.rearrange("(p j) m -> p j m", j=PACK))
            raw[g] = t

        def load_x(d):
            t = xr_pool.tile([P, N_OUT], BF16, name="xr")
            nc.sync.dma_start(out=t[:], in_=(Xd[d] if d < 8 else FF))
            x_raw[d] = t

        def interleave(copy, dst, src, m0, lo, hi):
            if hi > lo:
                copy(
                    out=dst[:, lo:hi, :].rearrange("p (c i) t -> p c t i", i=4),
                    in_=src[:, :, m0 + lo : m0 + hi].rearrange("p t (c i) -> p c t i", i=4),
                )

        def copy_w(i):
            g, m0, width, v_cols = units[i]
            t = grp_pool.tile([P, width, PACK], BF16, name="grp", align_bytes=64)
            interleave(nc.vector.tensor_copy, t, raw[g], m0, 0, v_cols)
            interleave(nc.scalar.copy, t, raw[g], m0, v_cols, width)
            grouped[i] = t

        def quant_w(i):
            width = units[i][2]
            c = wq_pool.tile([P, width], U32, name="wc", align_bytes=64)
            s = wq_pool.tile([P, width], U8, name="ws", align_bytes=64)
            nc.vector.quantize_mx(
                out=c[:].bitcast(FP8X4),
                scales=s[:],
                in_=grouped[i][:].rearrange("p m j -> p (m j)"),
            )
            w_codes[i] = c
            w_scales[i] = s

        def mm(i):
            g, m0, width, v_cols = units[i]
            d, h = g // 2, g % 2
            b_cols = slice(P * h, P * (h + 1))
            for n0 in range(0, width, N_GRP):
                n_cols = slice(n0, n0 + N_GRP)
                nc.tensor.matmul_mx(
                    out=acc[(m0 + n0) // N_GRP][:],
                    lhsT=x_codes[d][:, b_cols].bitcast(FP8X4),
                    lhsT_scale=x_scales[d][:, b_cols],
                    rhs=w_codes[i][:, n_cols].bitcast(FP8X4),
                    rhs_scale=w_scales[i][:, n_cols],
                    start=(g == 0),
                    stop=(g == PASSES - 1),
                )

        def xpose(d):
            t = xt_pool.tile([P, 2, 2, P], F32, name="xt")
            words = x_raw[d][:].bitcast(F32)
            for h in range(2):
                for u in range(2):
                    nc.tensor.transpose(
                        t[:, h, u, :], words[:, 256 * h + u : 256 * (h + 1) : 2], ident[:]
                    )
            x_t[d] = t

        def xevac(d):
            t = xg_pool.tile([P, 2, P, PACK], BF16, name="xg", align_bytes=64)
            nc.scalar.copy(out=t[:].bitcast(F32), in_=x_t[d][:].rearrange("p h u b -> p h b u"))
            x_grp[d] = t

        def xquant(d):
            c = xq_pool.tile([P, 2 * P], U32, name="xc", align_bytes=64)
            s = xq_pool.tile([P, 2 * P], U8, name="xs", align_bytes=64)
            nc.vector.quantize_mx(
                out=c[:].bitcast(FP8X4),
                scales=s[:],
                in_=x_grp[d][:].rearrange("p h b t -> p (h b t)"),
            )
            x_codes[d] = c
            x_scales[d] = s

        warm = const.tile([P, 1], F32, name="warm")
        nc.gpsimd.memset(warm[:], 0.0)
        warm2 = const.tile([P, 1], F32, name="warm2")
        nc.scalar.activation(out=warm2[:], in_=warm[:], func=COPY, scale=1.0)
        ident = const.tile([P, P], F32, name="ident")
        masks.make_identity(nc, ident[:])

        acc = []
        for q in range(N_OUT // N_GRP):
            acc_q = acc_pool.tile([P, N_GRP], F32, name="acc%d" % q)
            acc.append(acc_q)

        a_sb = const.tile([P, N_OUT], BF16, name="a_sb")
        v_sb = const.tile([P, N_OUT], BF16, name="v_sb")
        dist = const.tile([P, N_OUT], F32, name="dist")
        spike = const.tile([P, N_OUT], F32, name="spike")
        v_keep = const.tile([P, N_OUT], F32, name="v_keep")
        a_new = const.tile([P, N_OUT], F32, name="a_new")
        v_new = const.tile([P, N_OUT], F32, name="v_new")
        spike8 = const.tile([P, N_OUT], FP8, name="spike8")
        a_new8 = const.tile([P, N_OUT], FP8, name="a_new8")
        v_new8 = const.tile([P, N_OUT], FP8, name="v_new8")

        nc.sync.dma_start(out=a_sb[:], in_=a)
        nc.sync.dma_start(out=v_sb[:], in_=V)
        load_w(0)
        load_x(0)
        for g in range(1, PASSES):
            if g % 2 == 0:
                load_x(g // 2)
            load_w(g)

        nc.vector.scalar_tensor_tensor(
            out=dist[:], in0=a_sb[:], scalar=-1.8, in1=v_sb[:], op0=ALU.mult, op1=ALU.add
        )
        nc.vector.tensor_scalar(out=spike[:], in0=dist[:], scalar1=1.0, scalar2=None, op0=ALU.is_gt)
        nc.vector.scalar_tensor_tensor(
            out=v_keep[:], in0=dist[:], scalar=1.0, in1=v_sb[:], op0=ALU.is_le, op1=ALU.mult
        )
        nc.vector.scalar_tensor_tensor(
            out=a_new[:], in0=a_sb[:], scalar=0.9, in1=spike[:], op0=ALU.mult, op1=ALU.add
        )

        def cast_store(plane, val, val8, cols):
            nc.scalar.activation(
                out=val8[:, cols], in_=val[:, cols], func=COPY, scale=190.0, saturate=False
            )
            nc.sync.dma_start(out=out_0[plane][:, cols], in_=val[:, cols])
            nc.sync.dma_start(out=out_1[plane][:, cols], in_=val8[:, cols].bitcast(U8))

        def finish(i):
            g, m0, width, v_cols = units[i]
            for n0 in range(m0, m0 + width, N_GRP):
                nc.vector.scalar_tensor_tensor(
                    out=v_new[:, n0 : n0 + N_GRP],
                    in0=v_keep[:, n0 : n0 + N_GRP],
                    scalar=0.95,
                    in1=acc[n0 // N_GRP][:],
                    op0=ALU.mult,
                    op1=ALU.add,
                )
            cast_store(1, v_new, v_new8, slice(m0, m0 + width))

        whole = slice(0, N_OUT)
        for step in range(n_units + FIN_LAG + 1):
            if step < n_units:
                copy_w(step)
            for d in range(PAIRS):
                if step == first_unit[2 * d]:
                    xpose(d)
                    xevac(d)
                if step == first_unit[2 * d] + 1:
                    xquant(d)
            if step == CAST_SPIKE_STEP:
                cast_store(0, spike, spike8, whole)
            if step == CAST_A_STEP:
                cast_store(2, a_new, a_new8, whole)
            if 1 <= step <= n_units:
                quant_w(step - 1)
                mm(step - 1)
            if FIN_LAG <= step < n_units + FIN_LAG and units[step - FIN_LAG][0] == PASSES - 1:
                finish(step - FIN_LAG)
